import numpy as np
import ml_dtypes


def mxq(x, axis, fmt="e4m3"):
    dtype, down = {"e4m3": (ml_dtypes.float8_e4m3fn, 7), "e5m2": (ml_dtypes.float8_e5m2, 14)}[fmt]
    v = np.moveaxis(np.asarray(x, np.float32).astype(ml_dtypes.bfloat16).astype(np.float64), axis, -1)
    blocks = v.reshape(v.shape[:-1] + (-1, 32))
    amax = np.abs(blocks).max(-1, keepdims=True)
    byte = np.maximum(np.where(amax > 0, np.frexp(amax)[1] - 1 + 127, 0) - down, 1)
    scale = np.exp2(byte - 127.0)
    codes = (blocks / scale).astype(np.float32).astype(dtype).astype(np.float64)
    return np.moveaxis((codes * scale).reshape(v.shape), -1, axis)


WIDE = False


def mx_kscale(k):
    if not WIDE:
        return np.ones(k)
    levels = np.array([10, -10, 5, -5, 0])
    if k % 512:
        return np.exp2(np.random.permutation(np.resize(levels, k // 32))).repeat(32)
    a = np.empty((k // 512, 16))
    for p in range(k // 512):
        a[p, :8] = np.random.permutation(np.resize(levels, 8))
        for g in range(8):
            far = levels[np.abs(levels - a[p, g]) >= 10]
            a[p, g + 8] = far[np.random.randint(len(far))]
    return np.exp2(a.ravel()).repeat(32)


BF16 = ml_dtypes.bfloat16


def bf(x):
    return np.asarray(x, np.float32).astype(BF16)


def f64(x):
    return np.asarray(x).astype(np.float64)


B, S, D, BD, K = 4, 128, 512, 512, 128
TS = 3.0


def sigmoid(v):
    return 1.0 / (1.0 + np.exp(-v))


def setup_inputs():
    s = mx_kscale(D)
    return {
        "token_embeddings": bf(np.random.standard_normal((B, S, D)) * TS * s),
        "splat_influences": bf(np.random.uniform(size=(B, S, K))),
        "decoded": bf(np.random.standard_normal((B, K, D)) * 0.35),
        "gate_W": bf(np.random.standard_normal((D, D)) / (TS * np.sqrt(D)) / s[:, None]),
        "gate_b": bf(np.random.standard_normal(D) * 0.5),
    }


def reference(token_embeddings, splat_influences, decoded, gate_W, gate_b):
    flow = f64(splat_influences) @ f64(decoded)
    gate = sigmoid((mxq(f64(token_embeddings), 2, "e4m3") @ mxq(f64(gate_W), 0, "e4m3")) + f64(gate_b))
    return flow * gate

@@ -1,0 +1,141 @@
+from contextlib import ExitStack
+
+import concourse.mybir as mybir
+from concourse.masks import make_identity
+
+F32 = mybir.dt.float32
+BF16 = mybir.dt.bfloat16
+U32 = mybir.dt.uint32
+U8 = mybir.dt.uint8
+I32 = mybir.dt.int32
+FP8X4 = mybir.dt.float8_e4m3fn_x4
+ADD = mybir.AluOpType.add
+MULT = mybir.AluOpType.mult
+SIGMOID = mybir.ActivationFunctionType.Sigmoid
+
+P = 128
+B = 4
+D = 512
+PACK = 4
+HALVES = 2
+LAG = 2
+BANKS = 8
+ROWS = B
+W_PARTS = 2
+
+FLOPS = 2 * B * P * D * D + 2 * B * P * P * D
+
+
+def tile_splatinformationflow_pb_s_kernel(
+    tc, token_embeddings, splat_influences, decoded, gate_W, gate_b, out
+):
+    nc = tc.nc
+    with ExitStack() as ctx:
+        keep = ctx.enter_context(tc.tile_pool(name="keep", bufs=1))
+        work = ctx.enter_context(tc.tile_pool(name="work", bufs=B))
+        psum = ctx.enter_context(tc.psum_pool(name="psum", bufs=BANKS))
+        ctx.enter_context(tc.manual_schedule())
+
+        w_rows = keep.tile([P, PACK, D], BF16)
+        nc.sync.dma_start(out=w_rows[:], in_=gate_W.rearrange("(p t) n -> p t n", t=PACK))
+        bias_row = keep.tile([P, D], BF16)
+        nc.vector.memset(bias_row[:].bitcast(I32), 0)
+        nc.sync.dma_start(out=bias_row[0:1, :], in_=gate_b.rearrange("(o n) -> o n", o=1))
+        x_rows = keep.tile([P, B * D], BF16)
+        for b in range(B):
+            nc.sync.dma_start(out=x_rows[:, b * D : (b + 1) * D], in_=token_embeddings[b])
+        infl_rows = keep.tile([P, ROWS, P], BF16)
+        nc.sync.dma_start(
+            out=infl_rows[:], in_=splat_influences.flatten_outer_dims().rearrange("(p r) k -> p r k", r=ROWS)
+        )
+        dec_rows = keep.tile([P, B, D], BF16)
+        nc.sync.dma_start(out=dec_rows[:], in_=decoded.rearrange("b k d -> k b d"))
+
+        warm = keep.tile([P, 1], F32)
+        nc.vector.memset(warm[:], 0.0)
+        nc.scalar.activation(out=warm[:], in_=warm[:], func=SIGMOID)
+        ident_f32 = keep.tile([P, P], F32)
+        make_identity(nc, ident_f32[:])
+        ident_bf16 = keep.tile([P, P], BF16)
+        make_identity(nc, ident_bf16[:])
+
+        ones = keep.tile([P, P], BF16)
+        nc.vector.memset(ones[:], 1.0)
+        bias_ps = psum.tile([P, D], F32, tag="bank")
+        nc.tensor.matmul(out=bias_ps[:], lhsT=ones[:], rhs=bias_row[:], start=True, stop=True)
+        bias_all = keep.tile([P, D], F32)
+        nc.scalar.copy(out=bias_all[:], in_=bias_ps[:])
+
+        w_grouped = keep.tile([P, D, PACK], BF16, align_bytes=64)
+        w_codes = keep.tile([P, D], U32, align_bytes=64)
+        w_scales = keep.tile([P, D], U8, align_bytes=64)
+        w_cols = [slice(c * D // W_PARTS, (c + 1) * D // W_PARTS) for c in range(W_PARTS)]
+        for cols in w_cols:
+            nc.vector.tensor_copy(
+                out=w_grouped[:, cols, :].rearrange("p (c i) t -> p c t i", i=4),
+                in_=w_rows[:, :, cols].rearrange("p t (c i) -> p c t i", i=4),
+            )
+        for cols in w_cols:
+            nc.vector.quantize_mx(
+                out=w_codes[:, cols].bitcast(FP8X4),
+                scales=w_scales[:, cols],
+                in_=w_grouped[:, cols, :].rearrange("p n t -> p (n t)"),
+            )
+
+        x_words = x_rows[:].bitcast(F32)
+        x_grouped = keep.tile([P, B * P * PACK], BF16, align_bytes=64)
+        x_grouped_words = x_grouped[:].bitcast(F32)
+        x_codes = keep.tile([P, B * P], U32, align_bytes=64)
+        x_scales = keep.tile([P, B * P], U8, align_bytes=64)
+        for b in range(B):
+            xt_ps = psum.tile([P, HALVES, P], F32, tag="bank")
+            for u in range(HALVES):
+                words = x_words[:, b * HALVES * P + u : (b + 1) * HALVES * P : HALVES]
+                nc.tensor.transpose(xt_ps[:, u, :], words, ident_f32[:])
+            nc.scalar.copy(
+                out=x_grouped_words[:, b * P * HALVES : (b + 1) * P * HALVES].rearrange("p (s u) -> p s u", u=HALVES),
+                in_=xt_ps[:].rearrange("p u s -> p s u"),
+            )
+            nc.vector.quantize_mx(
+                out=x_codes[:, b * P : (b + 1) * P].bitcast(FP8X4),
+                scales=x_scales[:, b * P : (b + 1) * P],
+                in_=x_grouped[:, b * P * PACK : (b + 1) * P * PACK],
+            )
+
+        inflT_ps = psum.tile([P, ROWS, P], BF16, tag="bank")
+        for r in range(ROWS):
+            nc.tensor.transpose(inflT_ps[:, r, :], infl_rows[:, r, :], ident_bf16[:])
+        inflT = keep.tile([P, B * P], BF16)
+        nc.scalar.copy(out=inflT[:].rearrange("k (p r) -> k p r", r=ROWS), in_=inflT_ps[:].rearrange("k r p -> k p r"))
+
+        gates = []
+
+        def gate_of(b):
+            gate_ps = psum.tile([P, D], F32, tag="bank")
+            nc.tensor.matmul_mx(
+                out=gate_ps[:],
+                lhsT=x_codes[:, b * P : (b + 1) * P].bitcast(FP8X4),
+                lhsT_scale=x_scales[:, b * P : (b + 1) * P],
+                rhs=w_codes[:].bitcast(FP8X4),
+                rhs_scale=w_scales[:],
+                start=True,
+                stop=True,
+            )
+            logits = work.tile([P, D], F32)
+            nc.vector.tensor_tensor(out=logits[:], in0=gate_ps[:], in1=bias_all[:], op=ADD)
+            gate = work.tile([P, D], F32)
+            nc.scalar.activation(out=gate[:], in_=logits[:], func=SIGMOID)
+            gates.append(gate)
+
+        def gated_flow_of(b):
+            flow_ps = psum.tile([P, D], F32, tag="bank")
+            nc.tensor.matmul(out=flow_ps[:], lhsT=inflT[:, b * P : (b + 1) * P], rhs=dec_rows[:, b, :], start=True, stop=True)
+            result = work.tile([P, D], F32)
+            nc.vector.tensor_tensor(out=result[:], in0=flow_ps[:], in1=gates[b][:], op=MULT)
+            nc.sync.dma_start(out=out[b], in_=result[:])
+
+        for b in range(B + LAG):
+            if b < B:
+                gate_of(b)
+            if b >= LAG:
+                gated_flow_of(b - LAG)

@@ -59,19 +59,16 @@ def tile_splatinformationflow_pb_s_kernel(
         ident_bf16 = keep.tile([P, P], BF16)
         make_identity(nc, ident_bf16[:])
 
-        ones = keep.tile([P, P], BF16)
-        nc.vector.memset(ones[:], 1.0)
-        bias_ps = psum.tile([P, D], F32, tag="bank")
-        nc.tensor.matmul(out=bias_ps[:], lhsT=ones[:], rhs=bias_row[:], start=True, stop=True)
-        bias_all = keep.tile([P, D], F32)
-        nc.scalar.copy(out=bias_all[:], in_=bias_ps[:])
-
         w_grouped = keep.tile([P, D, PACK], BF16, align_bytes=64)
         w_codes = keep.tile([P, D], U32, align_bytes=64)
         w_scales = keep.tile([P, D], U8, align_bytes=64)
         w_cols = [slice(c * D // W_PARTS, (c + 1) * D // W_PARTS) for c in range(W_PARTS)]
-        for cols in w_cols:
-            nc.vector.tensor_copy(
+        for copy, cols in (
+            (nc.vector.tensor_copy, w_cols[0]),
+            (nc.vector.tensor_copy, slice(D // 2, 3 * D // 4)),
+            (nc.scalar.copy, slice(3 * D // 4, D)),
+        ):
+            copy(
                 out=w_grouped[:, cols, :].rearrange("p (c i) t -> p c t i", i=4),
                 in_=w_rows[:, :, cols].rearrange("p t (c i) -> p c t i", i=4),
             )
@@ -81,6 +78,13 @@ def tile_splatinformationflow_pb_s_kernel(
                 scales=w_scales[:, cols],
                 in_=w_grouped[:, cols, :].rearrange("p n t -> p (n t)"),
             )
+
+        ones = keep.tile([P, P], BF16)
+        nc.vector.memset(ones[:], 1.0)
+        bias_ps = psum.tile([P, D], F32, tag="bank")
+        nc.tensor.matmul(out=bias_ps[:], lhsT=ones[:], rhs=bias_row[:], start=True, stop=True)
+        bias_all = keep.tile([P, D], F32)
+        nc.scalar.copy(out=bias_all[:], in_=bias_ps[:])
 
         x_words = x_rows[:].bitcast(F32)
         x_grouped = keep.tile([P, B * P * PACK], BF16, align_bytes=64)

@@ -21,6 +21,8 @@ HALVES = 2
 LAG = 2
 BANKS = 8
 ROWS = B
+WARM_PASSES = 12
+EARLY = 2
 W_PARTS = 2
 
 FLOPS = 2 * B * P * D * D + 2 * B * P * P * D
@@ -38,8 +40,22 @@ def tile_splatinformationflow_pb_s_kernel(
 
         w_rows = keep.tile([P, PACK, D], BF16)
         nc.sync.dma_start(out=w_rows[:], in_=gate_W.rearrange("(p t) n -> p t n", t=PACK))
-        bias_row = keep.tile([P, D], BF16)
+        bias_row = keep.tile([P, D], BF16, align_bytes=64)
         nc.vector.memset(bias_row[:].bitcast(I32), 0)
+        warm_codes = keep.tile([P, P], U32, align_bytes=64)
+        warm_scales = keep.tile([P, P], U8, align_bytes=64)
+        nc.vector.quantize_mx(out=warm_codes[:].bitcast(FP8X4), scales=warm_scales[:], in_=bias_row[:])
+        warm_ps = psum.tile([P, D], F32, tag="bank")
+        for i in range(WARM_PASSES):
+            nc.tensor.matmul_mx(
+                out=warm_ps[:, 0:P],
+                lhsT=warm_codes[:].bitcast(FP8X4),
+                lhsT_scale=warm_scales[:],
+                rhs=warm_codes[:].bitcast(FP8X4),
+                rhs_scale=warm_scales[:],
+                start=True,
+                stop=True,
+            )
         nc.sync.dma_start(out=bias_row[0:1, :], in_=gate_b.rearrange("(o n) -> o n", o=1))
         x_rows = keep.tile([P, B * D], BF16)
         for b in range(B):
@@ -54,6 +70,9 @@ def tile_splatinformationflow_pb_s_kernel(
         warm = keep.tile([P, 1], F32)
         nc.vector.memset(warm[:], 0.0)
         nc.scalar.activation(out=warm[:], in_=warm[:], func=SIGMOID)
+        ones = keep.tile([P, P], BF16)
+        nc.vector.memset(ones[:], 1.0)
+
         ident_f32 = keep.tile([P, P], F32)
         make_identity(nc, ident_f32[:])
         ident_bf16 = keep.tile([P, P], BF16)
@@ -79,18 +98,23 @@ def tile_splatinformationflow_pb_s_kernel(
                 in_=w_grouped[:, cols, :].rearrange("p n t -> p (n t)"),
             )
 
-        ones = keep.tile([P, P], BF16)
-        nc.vector.memset(ones[:], 1.0)
         bias_ps = psum.tile([P, D], F32, tag="bank")
         nc.tensor.matmul(out=bias_ps[:], lhsT=ones[:], rhs=bias_row[:], start=True, stop=True)
         bias_all = keep.tile([P, D], F32)
-        nc.scalar.copy(out=bias_all[:], in_=bias_ps[:])
 
         x_words = x_rows[:].bitcast(F32)
         x_grouped = keep.tile([P, B * P * PACK], BF16, align_bytes=64)
         x_grouped_words = x_grouped[:].bitcast(F32)
         x_codes = keep.tile([P, B * P], U32, align_bytes=64)
         x_scales = keep.tile([P, B * P], U8, align_bytes=64)
+
+        def quantize_embeddings(b):
+            nc.vector.quantize_mx(
+                out=x_codes[:, b * P : (b + 1) * P].bitcast(FP8X4),
+                scales=x_scales[:, b * P : (b + 1) * P],
+                in_=x_grouped[:, b * P * PACK : (b + 1) * P * PACK],
+            )
+
         for b in range(B):
             xt_ps = psum.tile([P, HALVES, P], F32, tag="bank")
             for u in range(HALVES):
@@ -100,21 +124,24 @@ def tile_splatinformationflow_pb_s_kernel(
                 out=x_grouped_words[:, b * P * HALVES : (b + 1) * P * HALVES].rearrange("p (s u) -> p s u", u=HALVES),
                 in_=xt_ps[:].rearrange("p u s -> p s u"),
             )
-            nc.vector.quantize_mx(
-                out=x_codes[:, b * P : (b + 1) * P].bitcast(FP8X4),
-                scales=x_scales[:, b * P : (b + 1) * P],
-                in_=x_grouped[:, b * P * PACK : (b + 1) * P * PACK],
-            )
+            if b == 1:
+                nc.scalar.copy(out=bias_all[:], in_=bias_ps[:])
+            if b < EARLY:
+                quantize_embeddings(b)
 
-        inflT_ps = psum.tile([P, ROWS, P], BF16, tag="bank")
-        for r in range(ROWS):
-            nc.tensor.transpose(inflT_ps[:, r, :], infl_rows[:, r, :], ident_bf16[:])
         inflT = keep.tile([P, B * P], BF16)
-        nc.scalar.copy(out=inflT[:].rearrange("k (p r) -> k p r", r=ROWS), in_=inflT_ps[:].rearrange("k r p -> k p r"))
-
+        sums = []
         gates = []
 
-        def gate_of(b):
+        def turn_influences():
+            inflT_ps = psum.tile([P, ROWS, P], BF16, tag="bank")
+            for r in range(ROWS):
+                nc.tensor.transpose(inflT_ps[:, r, :], infl_rows[:, r, :], ident_bf16[:])
+            nc.scalar.copy(
+                out=inflT[:].rearrange("k (p r) -> k p r", r=ROWS), in_=inflT_ps[:].rearrange("k r p -> k p r")
+            )
+
+        def gate_sum_of(b):
             gate_ps = psum.tile([P, D], F32, tag="bank")
             nc.tensor.matmul_mx(
                 out=gate_ps[:],
@@ -127,8 +154,11 @@ def tile_splatinformationflow_pb_s_kernel(
             )
             logits = work.tile([P, D], F32)
             nc.vector.tensor_tensor(out=logits[:], in0=gate_ps[:], in1=bias_all[:], op=ADD)
+            sums.append(logits)
+
+        def gate_of(b):
             gate = work.tile([P, D], F32)
-            nc.scalar.activation(out=gate[:], in_=logits[:], func=SIGMOID)
+            nc.scalar.activation(out=gate[:], in_=sums[b][:], func=SIGMOID)
             gates.append(gate)
 
         def gated_flow_of(b):
@@ -139,6 +169,12 @@ def tile_splatinformationflow_pb_s_kernel(
             nc.sync.dma_start(out=out[b], in_=result[:])
 
         for b in range(B + LAG):
+            if b < B:
+                gate_sum_of(b)
+            if b == 0:
+                for later in range(EARLY, B):
+                    quantize_embeddings(later)
+                turn_influences()
             if b < B:
                 gate_of(b)
             if b >= LAG:

@@ -65,7 +65,8 @@ def tile_splatinformationflow_pb_s_kernel(
             out=infl_rows[:], in_=splat_influences.flatten_outer_dims().rearrange("(p r) k -> p r k", r=ROWS)
         )
         dec_rows = keep.tile([P, B, D], BF16)
-        nc.sync.dma_start(out=dec_rows[:], in_=decoded.rearrange("b k d -> k b d"))
+        for b in range(B):
+            nc.sync.dma_start(out=dec_rows[:, b, :], in_=decoded[b])
 
         warm = keep.tile([P, 1], F32)
         nc.vector.memset(warm[:], 0.0)

@@ -22,6 +22,7 @@ LAG = 2
 BANKS = 8
 ROWS = B
 WARM_PASSES = 12
+BIAS_AT = 2
 EARLY = 2
 W_PARTS = 2
 
@@ -56,9 +57,10 @@ def tile_splatinformationflow_pb_s_kernel(
                 start=True,
                 stop=True,
             )
-        nc.sync.dma_start(out=bias_row[0:1, :], in_=gate_b.rearrange("(o n) -> o n", o=1))
         x_rows = keep.tile([P, B * D], BF16)
         for b in range(B):
+            if b == BIAS_AT:
+                nc.sync.dma_start(out=bias_row[0:1, :], in_=gate_b.rearrange("(o n) -> o n", o=1))
             nc.sync.dma_start(out=x_rows[:, b * D : (b + 1) * D], in_=token_embeddings[b])
         infl_rows = keep.tile([P, ROWS, P], BF16)
         nc.sync.dma_start(
@@ -99,8 +101,6 @@ def tile_splatinformationflow_pb_s_kernel(
                 in_=w_grouped[:, cols, :].rearrange("p n t -> p (n t)"),
             )
 
-        bias_ps = psum.tile([P, D], F32, tag="bank")
-        nc.tensor.matmul(out=bias_ps[:], lhsT=ones[:], rhs=bias_row[:], start=True, stop=True)
         bias_all = keep.tile([P, D], F32)
 
         x_words = x_rows[:].bitcast(F32)
@@ -117,6 +117,10 @@ def tile_splatinformationflow_pb_s_kernel(
             )
 
         for b in range(B):
+            if b == BIAS_AT:
+                bias_ps = psum.tile([P, D], F32, tag="bank")
+                nc.tensor.matmul(out=bias_ps[:], lhsT=ones[:], rhs=bias_row[:], start=True, stop=True)
+                nc.scalar.copy(out=bias_all[:], in_=bias_ps[:])
             xt_ps = psum.tile([P, HALVES, P], F32, tag="bank")
             for u in range(HALVES):
                 words = x_words[:, b * HALVES * P + u : (b + 1) * HALVES * P : HALVES]
@@ -125,8 +129,6 @@ def tile_splatinformationflow_pb_s_kernel(
                 out=x_grouped_words[:, b * P * HALVES : (b + 1) * P * HALVES].rearrange("p (s u) -> p s u", u=HALVES),
                 in_=xt_ps[:].rearrange("p u s -> p s u"),
             )
-            if b == 1:
-                nc.scalar.copy(out=bias_all[:], in_=bias_ps[:])
             if b < EARLY:
                 quantize_embeddings(b)
 

from contextlib import ExitStack

import concourse.mybir as mybir
from concourse.masks import make_identity

F32 = mybir.dt.float32
BF16 = mybir.dt.bfloat16
U32 = mybir.dt.uint32
U8 = mybir.dt.uint8
I32 = mybir.dt.int32
FP8X4 = mybir.dt.float8_e4m3fn_x4
ADD = mybir.AluOpType.add
MULT = mybir.AluOpType.mult
SIGMOID = mybir.ActivationFunctionType.Sigmoid

P = 128
B = 4
D = 512
PACK = 4
HALVES = 2
LAG = 2
BANKS = 8
ROWS = B
WARM_PASSES = 12
BIAS_AT = 2
EARLY = 2
W_PARTS = 2

FLOPS = 2 * B * P * D * D + 2 * B * P * P * D


def tile_splatinformationflow_pb_s_kernel(
    tc, token_embeddings, splat_influences, decoded, gate_W, gate_b, out
):
    nc = tc.nc
    with ExitStack() as ctx:
        keep = ctx.enter_context(tc.tile_pool(name="keep", bufs=1))
        work = ctx.enter_context(tc.tile_pool(name="work", bufs=B))
        psum = ctx.enter_context(tc.psum_pool(name="psum", bufs=BANKS))
        ctx.enter_context(tc.manual_schedule())

        w_rows = keep.tile([P, PACK, D], BF16)
        nc.sync.dma_start(out=w_rows[:], in_=gate_W.rearrange("(p t) n -> p t n", t=PACK))
        bias_row = keep.tile([P, D], BF16, align_bytes=64)
        nc.vector.memset(bias_row[:].bitcast(I32), 0)
        warm_codes = keep.tile([P, P], U32, align_bytes=64)
        warm_scales = keep.tile([P, P], U8, align_bytes=64)
        nc.vector.quantize_mx(out=warm_codes[:].bitcast(FP8X4), scales=warm_scales[:], in_=bias_row[:])
        warm_ps = psum.tile([P, D], F32, tag="bank")
        for i in range(WARM_PASSES):
            nc.tensor.matmul_mx(
                out=warm_ps[:, 0:P],
                lhsT=warm_codes[:].bitcast(FP8X4),
                lhsT_scale=warm_scales[:],
                rhs=warm_codes[:].bitcast(FP8X4),
                rhs_scale=warm_scales[:],
                start=True,
                stop=True,
            )
        x_rows = keep.tile([P, B * D], BF16)
        for b in range(B):
            if b == BIAS_AT:
                nc.sync.dma_start(out=bias_row[0:1, :], in_=gate_b.rearrange("(o n) -> o n", o=1))
            nc.sync.dma_start(out=x_rows[:, b * D : (b + 1) * D], in_=token_embeddings[b])
        infl_rows = keep.tile([P, ROWS, P], BF16)
        nc.sync.dma_start(
            out=infl_rows[:], in_=splat_influences.flatten_outer_dims().rearrange("(p r) k -> p r k", r=ROWS)
        )
        dec_rows = keep.tile([P, B, D], BF16)
        for b in range(B):
            nc.sync.dma_start(out=dec_rows[:, b, :], in_=decoded[b])

        warm = keep.tile([P, 1], F32)
        nc.vector.memset(warm[:], 0.0)
        nc.scalar.activation(out=warm[:], in_=warm[:], func=SIGMOID)
        ones = keep.tile([P, P], BF16)
        nc.vector.memset(ones[:], 1.0)

        ident_f32 = keep.tile([P, P], F32)
        make_identity(nc, ident_f32[:])
        ident_bf16 = keep.tile([P, P], BF16)
        make_identity(nc, ident_bf16[:])

        w_grouped = keep.tile([P, D, PACK], BF16, align_bytes=64)
        w_codes = keep.tile([P, D], U32, align_bytes=64)
        w_scales = keep.tile([P, D], U8, align_bytes=64)
        w_cols = [slice(c * D // W_PARTS, (c + 1) * D // W_PARTS) for c in range(W_PARTS)]
        for copy, cols in (
            (nc.vector.tensor_copy, w_cols[0]),
            (nc.vector.tensor_copy, slice(D // 2, 3 * D // 4)),
            (nc.scalar.copy, slice(3 * D // 4, D)),
        ):
            copy(
                out=w_grouped[:, cols, :].rearrange("p (c i) t -> p c t i", i=4),
                in_=w_rows[:, :, cols].rearrange("p t (c i) -> p c t i", i=4),
            )
        for cols in w_cols:
            nc.vector.quantize_mx(
                out=w_codes[:, cols].bitcast(FP8X4),
                scales=w_scales[:, cols],
                in_=w_grouped[:, cols, :].rearrange("p n t -> p (n t)"),
            )

        bias_all = keep.tile([P, D], F32)

        x_words = x_rows[:].bitcast(F32)
        x_grouped = keep.tile([P, B * P * PACK], BF16, align_bytes=64)
        x_grouped_words = x_grouped[:].bitcast(F32)
        x_codes = keep.tile([P, B * P], U32, align_bytes=64)
        x_scales = keep.tile([P, B * P], U8, align_bytes=64)

        def quantize_embeddings(b):
            nc.vector.quantize_mx(
                out=x_codes[:, b * P : (b + 1) * P].bitcast(FP8X4),
                scales=x_scales[:, b * P : (b + 1) * P],
                in_=x_grouped[:, b * P * PACK : (b + 1) * P * PACK],
            )

        for b in range(B):
            if b == BIAS_AT:
                bias_ps = psum.tile([P, D], F32, tag="bank")
                nc.tensor.matmul(out=bias_ps[:], lhsT=ones[:], rhs=bias_row[:], start=True, stop=True)
                nc.scalar.copy(out=bias_all[:], in_=bias_ps[:])
            xt_ps = psum.tile([P, HALVES, P], F32, tag="bank")
            for u in range(HALVES):
                words = x_words[:, b * HALVES * P + u : (b + 1) * HALVES * P : HALVES]
                nc.tensor.transpose(xt_ps[:, u, :], words, ident_f32[:])
            nc.scalar.copy(
                out=x_grouped_words[:, b * P * HALVES : (b + 1) * P * HALVES].rearrange("p (s u) -> p s u", u=HALVES),
                in_=xt_ps[:].rearrange("p u s -> p s u"),
            )
            if b < EARLY:
                quantize_embeddings(b)

        inflT = keep.tile([P, B * P], BF16)
        sums = []
        gates = []

        def turn_influences():
            inflT_ps = psum.tile([P, ROWS, P], BF16, tag="bank")
            for r in range(ROWS):
                nc.tensor.transpose(inflT_ps[:, r, :], infl_rows[:, r, :], ident_bf16[:])
            nc.scalar.copy(
                out=inflT[:].rearrange("k (p r) -> k p r", r=ROWS), in_=inflT_ps[:].rearrange("k r p -> k p r")
            )

        def gate_sum_of(b):
            gate_ps = psum.tile([P, D], F32, tag="bank")
            nc.tensor.matmul_mx(
                out=gate_ps[:],
                lhsT=x_codes[:, b * P : (b + 1) * P].bitcast(FP8X4),
                lhsT_scale=x_scales[:, b * P : (b + 1) * P],
                rhs=w_codes[:].bitcast(FP8X4),
                rhs_scale=w_scales[:],
                start=True,
                stop=True,
            )
            logits = work.tile([P, D], F32)
            nc.vector.tensor_tensor(out=logits[:], in0=gate_ps[:], in1=bias_all[:], op=ADD)
            sums.append(logits)

        def gate_of(b):
            gate = work.tile([P, D], F32)
            nc.scalar.activation(out=gate[:], in_=sums[b][:], func=SIGMOID)
            gates.append(gate)

        def gated_flow_of(b):
            flow_ps = psum.tile([P, D], F32, tag="bank")
            nc.tensor.matmul(out=flow_ps[:], lhsT=inflT[:, b * P : (b + 1) * P], rhs=dec_rows[:, b, :], start=True, stop=True)
            result = work.tile([P, D], F32)
            nc.vector.tensor_tensor(out=result[:], in0=flow_ps[:], in1=gates[b][:], op=MULT)
            nc.sync.dma_start(out=out[b], in_=result[:])

        for b in range(B + LAG):
            if b < B:
                gate_sum_of(b)
            if b == 0:
                for later in range(EARLY, B):
                    quantize_embeddings(later)
                turn_influences()
            if b < B:
                gate_of(b)
            if b >= LAG:
                gated_flow_of(b - LAG)
